import numpy as np
import ml_dtypes


def mxq(x, axis, fmt="e4m3"):
    dtype, down = {"e4m3": (ml_dtypes.float8_e4m3fn, 7), "e5m2": (ml_dtypes.float8_e5m2, 14)}[fmt]
    v = np.moveaxis(np.asarray(x, np.float32).astype(ml_dtypes.bfloat16).astype(np.float64), axis, -1)
    blocks = v.reshape(v.shape[:-1] + (-1, 32))
    amax = np.abs(blocks).max(-1, keepdims=True)
    byte = np.maximum(np.where(amax > 0, np.frexp(amax)[1] - 1 + 127, 0) - down, 1)
    scale = np.exp2(byte - 127.0)
    codes = (blocks / scale).astype(np.float32).astype(dtype).astype(np.float64)
    return np.moveaxis((codes * scale).reshape(v.shape), -1, axis)


WIDE = False


def mx_kscale(k):
    if not WIDE:
        return np.ones(k)
    levels = np.array([10, -10, 5, -5, 0])
    a = np.random.permutation(np.resize(levels, k // 512 * 4)).reshape(k // 512, 4)
    idx = np.arange(k)
    return np.exp2(a[idx // 512, idx % 128 // 32])


BF16 = ml_dtypes.bfloat16


def bf(x):
    return np.asarray(x, np.float32).astype(BF16)


def f64(x):
    return np.asarray(x).astype(np.float64)


E2M1 = np.array([0.0, 0.5, 1.0, 1.5, 2.0, 3.0, 4.0, 6.0, -0.0, -0.5, -1.0, -1.5, -2.0, -3.0, -4.0, -6.0])


def pack_weight(w, fmt):
    k, n = w.shape
    w = f64(bf(w)).reshape(k // 32, 32, n)
    amax = np.abs(w).max(1)
    if fmt == "e4m3":
        byte = np.frexp(amax)[1] - 1 + 127 - 7
    else:
        mant, ex = np.frexp(amax / 6.0)
        byte = np.where(mant > 0.5, ex, ex - 1) + 127
    byte = np.clip(np.where(amax > 0, byte, 1), 1, 254)
    scaled = (w * np.exp2(127.0 - byte)[:, None, :]).reshape(k, n).astype(np.float32)
    by_word = np.ascontiguousarray(scaled.reshape(k // 512, 128, 4, n).transpose(0, 1, 3, 2))
    if fmt == "e4m3":
        words = by_word.astype(ml_dtypes.float8_e4m3fn).view(np.uint8)
    else:
        c = by_word.astype(ml_dtypes.float4_e2m1fn).view(np.uint8) & 0xF
        words = c[..., 0::2] | (c[..., 1::2] << 4)
    return np.ascontiguousarray(words), np.ascontiguousarray(byte.astype(np.uint8).reshape(k // 512, 16, n))


def unpack_weight(words, scales, fmt):
    g, p, n, _ = words.shape
    if fmt == "e4m3":
        vals = np.ascontiguousarray(words).view(ml_dtypes.float8_e4m3fn).astype(np.float64)
    else:
        nib = np.empty((g, p, n, 4), np.uint8)
        nib[..., 0::2] = words & 0xF
        nib[..., 1::2] = words >> 4
        vals = E2M1[nib]
    vals = vals * np.repeat(np.exp2(scales.astype(np.float64) - 127.0), 8, axis=1)[..., None]
    return vals.transpose(0, 1, 3, 2).reshape(g * 512, n)

def pack4(w):
    words, scales = pack_weight(w, "e2m1")
    return words.reshape(words.shape[0], 128, -1), scales


def unpack4(words, scales):
    return unpack_weight(words.reshape(words.shape[0], 128, -1, 2), scales, "e2m1")


B, C_IN, H, W, C_OUT = 2, 4096, 8, 8, 4096
E = 1


def _box_sum(x):
    b, h, w, c = x.shape
    xp = np.pad(x, ((0, 0), (1, 1), (1, 1), (0, 0)))
    out = np.zeros_like(x)
    for i in range(3):
        for j in range(3):
            out = out + xp[:, i:i + h, j:j + w, :]
    return out


def setup_inputs():
    s = mx_kscale(C_IN)
    x = bf(np.random.standard_normal((B, C_IN, H, W)) * s[None, :, None, None])
    stack = np.random.standard_normal((E, C_IN, C_OUT)) * 3.0 / np.sqrt(C_IN) / s[None, :, None]
    words, scales = pack4(stack.reshape(-1, C_OUT))
    return {"x": x, "weight_words": words, "weight_scales": scales}


def reference(x, weight_words, weight_scales):
    x = f64(x)
    weight = unpack4(weight_words, weight_scales).reshape(E, C_IN, C_OUT)
    b, c, h, w = x.shape
    o = weight.shape[-1]
    x1 = np.transpose(x, (0, 2, 3, 1))
    xw = mxq(x1, 3, "e4m3") @ weight[0]
    deg = _box_sum(np.ones((1, h, w, 1)))
    dinv = 1.0 / np.sqrt(deg)
    y = dinv * _box_sum(dinv * xw)
    return np.transpose(y, (0, 3, 1, 2)).reshape(b, o, w, h)

@@ -1,0 +1,180 @@
+from contextlib import ExitStack
+
+import concourse.mybir as mybir
+from concourse.masks import make_identity
+
+F32 = mybir.dt.float32
+BF16 = mybir.dt.bfloat16
+I32 = mybir.dt.int32
+U32 = mybir.dt.uint32
+U8 = mybir.dt.uint8
+FP8X4 = mybir.dt.float8_e4m3fn_x4
+FP4X4 = mybir.dt.float4_e2m1fn_x4
+MULT = mybir.AluOpType.mult
+
+P = 128
+PACK = 4
+K_PASS = P * PACK
+BATCH, C_IN, GRID, C_OUT = 2, 4096, 8, 4096
+CELLS = GRID * GRID
+TOKENS = BATCH * CELLS
+PASSES = C_IN // K_PASS
+HALF = PASSES // 2
+BANK = 512
+RANGE = 1024
+RANGES = C_OUT // RANGE
+BANKS = RANGE // BANK
+PER_PARTITION = RANGE // P
+PER_BANK = BANK // TOKENS
+SCALE_ROWS = K_PASS // 32
+
+FLOPS = 2 * TOKENS * C_IN * C_OUT + 2 * TOKENS * TOKENS * C_OUT
+
+
+def box_sum(nc, pool, images, count):
+    by_row = images.rearrange("p (r j) -> p r j", j=GRID)
+    row_sum = pool.tile([P, count * GRID, GRID], F32, name="row_sum")
+    nc.vector.tensor_copy(out=row_sum[:], in_=by_row)
+    nc.vector.tensor_add(out=row_sum[:, :, 1:], in0=row_sum[:, :, 1:], in1=by_row[:, :, : GRID - 1])
+    nc.vector.tensor_add(out=row_sum[:, :, : GRID - 1], in0=row_sum[:, :, : GRID - 1], in1=by_row[:, :, 1:])
+    by_image = row_sum[:].rearrange("p (n i) j -> p n (i j)", i=GRID)
+    box = pool.tile([P, count, CELLS], F32, name="box")
+    nc.vector.tensor_copy(out=box[:], in_=by_image)
+    nc.vector.tensor_add(out=box[:, :, GRID:], in0=box[:, :, GRID:], in1=by_image[:, :, : CELLS - GRID])
+    nc.vector.tensor_add(out=box[:, :, : CELLS - GRID], in0=box[:, :, : CELLS - GRID], in1=by_image[:, :, GRID:])
+    return box
+
+
+def load_range(nc, keep, weight_words, weight_scales, r):
+    cols = slice(r * RANGE, (r + 1) * RANGE)
+    planes = keep.tile([P, PASSES, RANGE], U8, name="planes%d" % r, align_bytes=64)
+    nc.vector.memset(planes[:].bitcast(I32), 0)
+    rows = weight_scales.rearrange("g q n -> q g n")
+    for quadrant in range(2):
+        for row in range(4):
+            q = 4 * quadrant + row
+            nc.sync.dma_start(
+                out=planes[32 * quadrant + row : P : 64, :, :].bitcast(I32),
+                in_=rows[q : SCALE_ROWS : 8, :, cols].bitcast(I32),
+            )
+    words = []
+    for g in range(PASSES):
+        words_g = keep.tile([P, 2 * RANGE], U8, name="words%d_%d" % (r, g), align_bytes=64)
+        nc.sync.dma_start(
+            out=words_g[:].bitcast(I32),
+            in_=weight_words[g, :, 2 * r * RANGE : 2 * (r + 1) * RANGE].bitcast(I32),
+        )
+        words.append(words_g)
+    return planes, words
+
+
+def tile_gcn_layer_w_e_kernel(tc, x, weight_words, weight_scales, out):
+    nc = tc.nc
+    with ExitStack() as ctx:
+        ctx.enter_context(tc.manual_schedule())
+        keep = ctx.enter_context(tc.tile_pool(name="keep", bufs=1))
+        stage = ctx.enter_context(tc.tile_pool(name="stage", bufs=2))
+        psum = ctx.enter_context(tc.psum_pool(name="psum", bufs=2))
+
+        x_raw = keep.tile([P, BATCH, PASSES, PACK * CELLS], BF16, name="x_raw")
+        for b in range(BATCH):
+            nc.sync.dma_start(
+                out=x_raw[:, b],
+                in_=x[b].rearrange("(g p t) i j -> p g (t i j)", g=PASSES, p=P, t=PACK),
+            )
+        loaded = [load_range(nc, keep, weight_words, weight_scales, 0)]
+
+        images = keep.tile([P, 2 * TOKENS], F32, name="images")
+        make_identity(nc, images[:, :TOKENS])
+        nc.gpsimd.memset(images[:, TOKENS:], 1.0)
+        box = box_sum(nc, keep, images[:], 2 * BATCH)
+        neighbours = box[:, :BATCH, :].rearrange("p b s -> p (b s)")
+        deg = box[:, BATCH:, :].rearrange("p b s -> p (b s)")
+        root = keep.tile([P, TOKENS], F32, name="root")
+        nc.scalar.sqrt(out=root[:], in_=deg)
+
+        grouped = keep.tile([P, PASSES, TOKENS, PACK], BF16, name="grouped", align_bytes=64)
+        x_codes = keep.tile([P, PASSES, TOKENS], U32, name="x_codes", align_bytes=64)
+        x_scales = keep.tile([P, PASSES, TOKENS], U8, name="x_scales", align_bytes=64)
+        for b in range(BATCH):
+            tokens = slice(b * CELLS, (b + 1) * CELLS)
+            nc.vector.tensor_copy(
+                out=grouped[:, :HALF, tokens, :],
+                in_=x_raw[:, b, :HALF, :].rearrange("p g (t s) -> p g s t", t=PACK),
+            )
+            nc.scalar.copy(
+                out=grouped[:, HALF:, tokens, :],
+                in_=x_raw[:, b, HALF:, :].rearrange("p g (t s) -> p g s t", t=PACK),
+            )
+
+        def quantise(passes):
+            nc.vector.quantize_mx(
+                out=x_codes[:, passes, :].rearrange("p g s -> p (g s)").bitcast(FP8X4),
+                scales=x_scales[:, passes, :].rearrange("p g s -> p (g s)"),
+                in_=grouped[:, passes, :, :].rearrange("p g s t -> p (g s t)"),
+            )
+
+        quantise(slice(0, HALF))
+
+        dinv_free = keep.tile([P, TOKENS], F32, name="dinv_free")
+        nc.vector.reciprocal(out=dinv_free[:], in_=root[:])
+        own = keep.tile([P, TOKENS], F32, name="own")
+        nc.vector.tensor_mul(out=own[:], in0=images[:, :TOKENS], in1=dinv_free[:])
+        dinv_part = keep.tile([P, 1], F32, name="dinv_part")
+        nc.vector.reduce_sum(out=dinv_part[:], in_=own[:], axis=mybir.AxisListType.X)
+        graph = keep.tile([P, TOKENS], F32, name="graph")
+        nc.vector.scalar_tensor_tensor(
+            out=graph[:], in0=neighbours, scalar=dinv_part[:], in1=dinv_free[:], op0=MULT, op1=MULT
+        )
+
+        quantise(slice(HALF, PASSES))
+
+        for r in range(1, RANGES):
+            loaded.append(load_range(nc, keep, weight_words, weight_scales, r))
+
+        for r in range(RANGES):
+            planes, words = loaded[r]
+            xw_banks = [psum.tile([P, BANK], F32, name="xw_bank%d" % c) for c in range(BANKS)]
+            for g in range(PASSES):
+                for c in range(BANKS):
+                    nc.tensor.matmul_mx(
+                        out=xw_banks[c][:],
+                        lhsT=x_codes[:, g, :].bitcast(FP8X4),
+                        lhsT_scale=x_scales[:, g, :],
+                        rhs=words[g][:, 2 * c * BANK : 2 * (c + 1) * BANK].bitcast(FP4X4),
+                        rhs_scale=planes[:, g, c * BANK : (c + 1) * BANK],
+                        start=(g == 0),
+                        stop=(g == PASSES - 1),
+                    )
+
+            xw = stage.tile([P, PER_PARTITION, P], F32, name="xw")
+            m_per_bank = BANK // PER_PARTITION
+            for c in range(BANKS):
+                copy = nc.vector.tensor_copy if c % 2 == 0 else nc.scalar.copy
+                copy(
+                    out=xw[:, :, c * m_per_bank : (c + 1) * m_per_bank],
+                    in_=xw_banks[c][:].rearrange("p (m t) -> p t m", t=PER_PARTITION),
+                )
+
+            y = keep.tile([P, BATCH, PER_PARTITION, CELLS], F32, name="y%d" % r)
+            for h in range(PER_PARTITION // PER_BANK):
+                y_bank = psum.tile([P, PER_BANK, TOKENS], F32, name="y_bank%d" % h)
+                for t in range(PER_BANK):
+                    nc.tensor.matmul(
+                        out=y_bank[:, t, :],
+                        lhsT=xw[:, h * PER_BANK + t, :],
+                        rhs=graph[:],
+                        start=True,
+                        stop=True,
+                    )
+                copy = nc.vector.tensor_copy if h % 2 == 0 else nc.scalar.copy
+                copy(
+                    out=y[:, :, h * PER_BANK : (h + 1) * PER_BANK, :],
+                    in_=y_bank[:].rearrange("m t (b s) -> m b t s", b=BATCH),
+                )
+            nc.sync.dma_start(
+                out=out[:, r * RANGE : (r + 1) * RANGE].rearrange(
+                    "b (m t) i j -> m b (t i j)", t=PER_PARTITION
+                ),
+                in_=y[:].rearrange("m b t s -> m b (t s)"),
+            )

@@ -27,6 +27,7 @@ BANKS = RANGE // BANK
 PER_PARTITION = RANGE // P
 PER_BANK = BANK // TOKENS
 SCALE_ROWS = K_PASS // 32
+EARLY = 2
 
 FLOPS = 2 * TOKENS * C_IN * C_OUT + 2 * TOKENS * TOKENS * C_OUT
 
@@ -50,13 +51,11 @@ def load_range(nc, keep, weight_words, weight_scales, r):
     planes = keep.tile([P, PASSES, RANGE], U8, name="planes%d" % r, align_bytes=64)
     nc.vector.memset(planes[:].bitcast(I32), 0)
     rows = weight_scales.rearrange("g q n -> q g n")
-    for quadrant in range(2):
-        for row in range(4):
-            q = 4 * quadrant + row
-            nc.sync.dma_start(
-                out=planes[32 * quadrant + row : P : 64, :, :].bitcast(I32),
-                in_=rows[q : SCALE_ROWS : 8, :, cols].bitcast(I32),
-            )
+    for row in range(4):
+        nc.sync.dma_start(
+            out=planes[row:P:32, :, :].bitcast(I32),
+            in_=rows[row:SCALE_ROWS:4, :, cols].bitcast(I32),
+        )
     words = []
     for g in range(PASSES):
         words_g = keep.tile([P, 2 * RANGE], U8, name="words%d_%d" % (r, g), align_bytes=64)
@@ -82,7 +81,7 @@ def tile_gcn_layer_w_e_kernel(tc, x, weight_words, weight_scales, out):
                 out=x_raw[:, b],
                 in_=x[b].rearrange("(g p t) i j -> p g (t i j)", g=PASSES, p=P, t=PACK),
             )
-        loaded = [load_range(nc, keep, weight_words, weight_scales, 0)]
+        loaded = [load_range(nc, keep, weight_words, weight_scales, r) for r in range(EARLY)]
 
         images = keep.tile([P, 2 * TOKENS], F32, name="images")
         make_identity(nc, images[:, :TOKENS])
@@ -129,7 +128,7 @@ def tile_gcn_layer_w_e_kernel(tc, x, weight_words, weight_scales, out):
 
         quantise(slice(HALF, PASSES))
 
-        for r in range(1, RANGES):
+        for r in range(EARLY, RANGES):
             loaded.append(load_range(nc, keep, weight_words, weight_scales, r))
 
         for r in range(RANGES):

@@ -24,8 +24,7 @@ BANK = 512
 RANGE = 1024
 RANGES = C_OUT // RANGE
 BANKS = RANGE // BANK
-PER_PARTITION = RANGE // P
-PER_BANK = BANK // TOKENS
+PER_PARTITION = BANK // P
 SCALE_ROWS = K_PASS // 32
 EARLY = 2
 
@@ -51,11 +50,13 @@ def load_range(nc, keep, weight_words, weight_scales, r):
     planes = keep.tile([P, PASSES, RANGE], U8, name="planes%d" % r, align_bytes=64)
     nc.vector.memset(planes[:].bitcast(I32), 0)
     rows = weight_scales.rearrange("g q n -> q g n")
-    for row in range(4):
-        nc.sync.dma_start(
-            out=planes[row:P:32, :, :].bitcast(I32),
-            in_=rows[row:SCALE_ROWS:4, :, cols].bitcast(I32),
-        )
+    for quadrant in range(2):
+        for row in range(4):
+            q = 4 * quadrant + row
+            nc.sync.dma_start(
+                out=planes[32 * quadrant + row : P : 64, :, :].bitcast(I32),
+                in_=rows[q : SCALE_ROWS : 8, :, cols].bitcast(I32),
+            )
     words = []
     for g in range(PASSES):
         words_g = keep.tile([P, 2 * RANGE], U8, name="words%d_%d" % (r, g), align_bytes=64)
@@ -146,34 +147,17 @@ def tile_gcn_layer_w_e_kernel(tc, x, weight_words, weight_scales, out):
                         stop=(g == PASSES - 1),
                     )
 
-            xw = stage.tile([P, PER_PARTITION, P], F32, name="xw")
-            m_per_bank = BANK // PER_PARTITION
             for c in range(BANKS):
                 copy = nc.vector.tensor_copy if c % 2 == 0 else nc.scalar.copy
-                copy(
-                    out=xw[:, :, c * m_per_bank : (c + 1) * m_per_bank],
-                    in_=xw_banks[c][:].rearrange("p (m t) -> p t m", t=PER_PARTITION),
+                first = r * RANGE + c * BANK
+                xw = stage.tile([P, PER_PARTITION, P], F32, name="xw%d" % c)
+                copy(out=xw[:], in_=xw_banks[c][:].rearrange("p (m t) -> p t m", t=PER_PARTITION))
+                y_bank = psum.tile([P, PER_PARTITION, TOKENS], F32, name="y_bank%d" % c)
+                for t in range(PER_PARTITION):
+                    nc.tensor.matmul(out=y_bank[:, t, :], lhsT=xw[:, t, :], rhs=graph[:], start=True, stop=True)
+                y = keep.tile([P, BATCH, PER_PARTITION, CELLS], F32, name="y%d_%d" % (r, c))
+                copy(out=y[:], in_=y_bank[:].rearrange("m t (b s) -> m b t s", b=BATCH))
+                nc.sync.dma_start(
+                    out=out[:, first : first + BANK].rearrange("b (m t) i j -> m b (t i j)", t=PER_PARTITION),
+                    in_=y[:].rearrange("m b t s -> m b (t s)"),
                 )
-
-            y = keep.tile([P, BATCH, PER_PARTITION, CELLS], F32, name="y%d" % r)
-            for h in range(PER_PARTITION // PER_BANK):
-                y_bank = psum.tile([P, PER_BANK, TOKENS], F32, name="y_bank%d" % h)
-                for t in range(PER_BANK):
-                    nc.tensor.matmul(
-                        out=y_bank[:, t, :],
-                        lhsT=xw[:, h * PER_BANK + t, :],
-                        rhs=graph[:],
-                        start=True,
-                        stop=True,
-                    )
-                copy = nc.vector.tensor_copy if h % 2 == 0 else nc.scalar.copy
-                copy(
-                    out=y[:, :, h * PER_BANK : (h + 1) * PER_BANK, :],
-                    in_=y_bank[:].rearrange("m t (b s) -> m b t s", b=BATCH),
-                )
-            nc.sync.dma_start(
-                out=out[:, r * RANGE : (r + 1) * RANGE].rearrange(
-                    "b (m t) i j -> m b (t i j)", t=PER_PARTITION
-                ),
-                in_=y[:].rearrange("m b t s -> m b (t s)"),
-            )

@@ -10,7 +10,6 @@ U32 = mybir.dt.uint32
 U8 = mybir.dt.uint8
 FP8X4 = mybir.dt.float8_e4m3fn_x4
 FP4X4 = mybir.dt.float4_e2m1fn_x4
-MULT = mybir.AluOpType.mult
 
 P = 128
 PACK = 4
@@ -27,6 +26,7 @@ BANKS = RANGE // BANK
 PER_PARTITION = BANK // P
 SCALE_ROWS = K_PASS // 32
 EARLY = 2
+INNER = 3
 
 FLOPS = 2 * TOKENS * C_IN * C_OUT + 2 * TOKENS * TOKENS * C_OUT
 
@@ -45,10 +45,14 @@ def box_sum(nc, pool, images, count):
     return box
 
 
-def load_range(nc, keep, weight_words, weight_scales, r):
-    cols = slice(r * RANGE, (r + 1) * RANGE)
-    planes = keep.tile([P, PASSES, RANGE], U8, name="planes%d" % r, align_bytes=64)
+def zero_planes(nc, keep, slot):
+    planes = keep.tile([P, PASSES, RANGE], U8, name="planes%d" % slot, align_bytes=64)
     nc.vector.memset(planes[:].bitcast(I32), 0)
+    return planes
+
+
+def load_range(nc, keep, weight_words, weight_scales, r, planes):
+    cols = slice(r * RANGE, (r + 1) * RANGE)
     rows = weight_scales.rearrange("g q n -> q g n")
     for quadrant in range(2):
         for row in range(4):
@@ -77,61 +81,65 @@ def tile_gcn_layer_w_e_kernel(tc, x, weight_words, weight_scales, out):
         psum = ctx.enter_context(tc.psum_pool(name="psum", bufs=2))
 
         x_raw = keep.tile([P, BATCH, PASSES, PACK * CELLS], BF16, name="x_raw")
-        for b in range(BATCH):
-            nc.sync.dma_start(
-                out=x_raw[:, b],
-                in_=x[b].rearrange("(g p t) i j -> p g (t i j)", g=PASSES, p=P, t=PACK),
-            )
-        loaded = [load_range(nc, keep, weight_words, weight_scales, r) for r in range(EARLY)]
+        for half in range(2):
+            passes = slice(half * HALF, (half + 1) * HALF)
+            for b in range(BATCH):
+                nc.sync.dma_start(
+                    out=x_raw[:, b, passes, :],
+                    in_=x[b].rearrange("(g p t) i j -> p g (t i j)", g=PASSES, p=P, t=PACK)[:, passes, :],
+                )
+        zeroed = [zero_planes(nc, keep, slot) for slot in range(EARLY)]
+        loaded = [load_range(nc, keep, weight_words, weight_scales, r, zeroed[r]) for r in range(EARLY)]
 
-        images = keep.tile([P, 2 * TOKENS], F32, name="images")
-        make_identity(nc, images[:, :TOKENS])
-        nc.gpsimd.memset(images[:, TOKENS:], 1.0)
-        box = box_sum(nc, keep, images[:], 2 * BATCH)
-        neighbours = box[:, :BATCH, :].rearrange("p b s -> p (b s)")
-        deg = box[:, BATCH:, :].rearrange("p b s -> p (b s)")
-        root = keep.tile([P, TOKENS], F32, name="root")
-        nc.scalar.sqrt(out=root[:], in_=deg)
+        identity = keep.tile([P, TOKENS], F32, name="identity")
+        dinv = keep.tile([P, BATCH, GRID, GRID], F32, name="dinv")
+        nc.gpsimd.memset(dinv[:], 1.0)
+        make_identity(nc, identity[:])
+        warm = keep.tile([P, 1], F32, name="warm")
+        nc.scalar.copy(out=warm[:], in_=dinv[:, 0, 0, :1])
 
         grouped = keep.tile([P, PASSES, TOKENS, PACK], BF16, name="grouped", align_bytes=64)
         x_codes = keep.tile([P, PASSES, TOKENS], U32, name="x_codes", align_bytes=64)
         x_scales = keep.tile([P, PASSES, TOKENS], U8, name="x_scales", align_bytes=64)
-        for b in range(BATCH):
-            tokens = slice(b * CELLS, (b + 1) * CELLS)
-            nc.vector.tensor_copy(
-                out=grouped[:, :HALF, tokens, :],
-                in_=x_raw[:, b, :HALF, :].rearrange("p g (t s) -> p g s t", t=PACK),
-            )
-            nc.scalar.copy(
-                out=grouped[:, HALF:, tokens, :],
-                in_=x_raw[:, b, HALF:, :].rearrange("p g (t s) -> p g s t", t=PACK),
+
+        def regroup(copy, half, b):
+            passes = slice(half * HALF, (half + 1) * HALF)
+            copy(
+                out=grouped[:, passes, b * CELLS : (b + 1) * CELLS, :],
+                in_=x_raw[:, b, passes, :].rearrange("p g (t s) -> p g s t", t=PACK),
             )
 
-        def quantise(passes):
+        def quantise(half):
+            passes = slice(half * HALF, (half + 1) * HALF)
             nc.vector.quantize_mx(
                 out=x_codes[:, passes, :].rearrange("p g s -> p (g s)").bitcast(FP8X4),
                 scales=x_scales[:, passes, :].rearrange("p g s -> p (g s)"),
                 in_=grouped[:, passes, :, :].rearrange("p g s t -> p (g s t)"),
             )
 
-        quantise(slice(0, HALF))
+        regroup(nc.vector.tensor_copy, 0, 0)
+        regroup(nc.vector.tensor_copy, 0, 1)
+        regroup(nc.scalar.copy, 1, 0)
+        quantise(0)
+        regroup(nc.vector.tensor_copy, 1, 1)
+        quantise(1)
 
-        dinv_free = keep.tile([P, TOKENS], F32, name="dinv_free")
-        nc.vector.reciprocal(out=dinv_free[:], in_=root[:])
-        own = keep.tile([P, TOKENS], F32, name="own")
-        nc.vector.tensor_mul(out=own[:], in0=images[:, :TOKENS], in1=dinv_free[:])
-        dinv_part = keep.tile([P, 1], F32, name="dinv_part")
-        nc.vector.reduce_sum(out=dinv_part[:], in_=own[:], axis=mybir.AxisListType.X)
-        graph = keep.tile([P, TOKENS], F32, name="graph")
-        nc.vector.scalar_tensor_tensor(
-            out=graph[:], in0=neighbours, scalar=dinv_part[:], in1=dinv_free[:], op0=MULT, op1=MULT
+        border = (INNER / (INNER - 1)) ** 0.5
+        nc.vector.tensor_scalar_mul(out=dinv[:], in0=dinv[:], scalar1=1.0 / INNER)
+        nc.vector.tensor_scalar_mul(
+            out=dinv[:, :, 0 : GRID : GRID - 1, :], in0=dinv[:, :, 0 : GRID : GRID - 1, :], scalar1=border
         )
+        nc.vector.tensor_scalar_mul(
+            out=dinv[:, :, :, 0 : GRID : GRID - 1], in0=dinv[:, :, :, 0 : GRID : GRID - 1], scalar1=border
+        )
+        dinv_flat = dinv[:].rearrange("p b i j -> p (b i j)")
+        own = keep.tile([P, TOKENS], F32, name="own")
+        nc.vector.tensor_mul(out=own[:], in0=identity[:], in1=dinv_flat)
+        box = box_sum(nc, keep, own[:], BATCH)
+        graph = keep.tile([P, TOKENS], F32, name="graph")
+        nc.vector.tensor_mul(out=graph[:], in0=box[:].rearrange("p b s -> p (b s)"), in1=dinv_flat)
 
-        quantise(slice(HALF, PASSES))
-
-        for r in range(EARLY, RANGES):
-            loaded.append(load_range(nc, keep, weight_words, weight_scales, r))
-
+        waiting = []
         for r in range(RANGES):
             planes, words = loaded[r]
             xw_banks = [psum.tile([P, BANK], F32, name="xw_bank%d" % c) for c in range(BANKS)]
@@ -147,6 +155,9 @@ def tile_gcn_layer_w_e_kernel(tc, x, weight_words, weight_scales, out):
                         stop=(g == PASSES - 1),
                     )
 
+            if r + EARLY < RANGES:
+                loaded.append(load_range(nc, keep, weight_words, weight_scales, r + EARLY, planes))
+
             for c in range(BANKS):
                 copy = nc.vector.tensor_copy if c % 2 == 0 else nc.scalar.copy
                 first = r * RANGE + c * BANK
@@ -157,7 +168,12 @@ def tile_gcn_layer_w_e_kernel(tc, x, weight_words, weight_scales, out):
                     nc.tensor.matmul(out=y_bank[:, t, :], lhsT=xw[:, t, :], rhs=graph[:], start=True, stop=True)
                 y = keep.tile([P, BATCH, PER_PARTITION, CELLS], F32, name="y%d_%d" % (r, c))
                 copy(out=y[:], in_=y_bank[:].rearrange("m t (b s) -> m b t s", b=BATCH))
-                nc.sync.dma_start(
-                    out=out[:, first : first + BANK].rearrange("b (m t) i j -> m b (t i j)", t=PER_PARTITION),
-                    in_=y[:].rearrange("m b t s -> m b (t s)"),
-                )
+                waiting.append((first, y))
+
+            if len(loaded) == RANGES:
+                for first, y in waiting:
+                    nc.sync.dma_start(
+                        out=out[:, first : first + BANK].rearrange("b (m t) i j -> m b (t i j)", t=PER_PARTITION),
+                        in_=y[:].rearrange("m b t s -> m b (t s)"),
+                    )
+                waiting.clear()

@@ -26,6 +26,7 @@ BANKS = RANGE // BANK
 PER_PARTITION = BANK // P
 SCALE_ROWS = K_PASS // 32
 EARLY = 2
+SPLIT = 2
 INNER = 3
 
 FLOPS = 2 * TOKENS * C_IN * C_OUT + 2 * TOKENS * TOKENS * C_OUT
@@ -61,15 +62,26 @@ def load_range(nc, keep, weight_words, weight_scales, r, planes):
                 out=planes[32 * quadrant + row : P : 64, :, :].bitcast(I32),
                 in_=rows[q : SCALE_ROWS : 8, :, cols].bitcast(I32),
             )
-    words = []
-    for g in range(PASSES):
-        words_g = keep.tile([P, 2 * RANGE], U8, name="words%d_%d" % (r, g), align_bytes=64)
-        nc.sync.dma_start(
-            out=words_g[:].bitcast(I32),
-            in_=weight_words[g, :, 2 * r * RANGE : 2 * (r + 1) * RANGE].bitcast(I32),
-        )
-        words.append(words_g)
+    words = {}
+    for g, banks in load_order(r):
+        width = 2 * BANK * len(banks)
+        start = 2 * (r * RANGE + banks[0] * BANK)
+        piece = keep.tile([P, width], U8, name="words%d_%d_%d" % (r, g, banks[0]), align_bytes=64)
+        nc.sync.dma_start(out=piece[:].bitcast(I32), in_=weight_words[g, :, start : start + width].bitcast(I32))
+        for i, c in enumerate(banks):
+            words[g, c] = piece[:, 2 * i * BANK : 2 * (i + 1) * BANK]
     return planes, words
+
+
+def load_order(r):
+    whole = PASSES - (SPLIT if r == RANGES - 1 else 0)
+    return [(g, list(range(BANKS))) for g in range(whole)] + [
+        (g, [c]) for c in range(BANKS) for g in range(whole, PASSES)
+    ]
+
+
+def pass_order(r):
+    return [(g, c) for g, banks in load_order(r) for c in banks]
 
 
 def tile_gcn_layer_w_e_kernel(tc, x, weight_words, weight_scales, out):
@@ -143,17 +155,16 @@ def tile_gcn_layer_w_e_kernel(tc, x, weight_words, weight_scales, out):
         for r in range(RANGES):
             planes, words = loaded[r]
             xw_banks = [psum.tile([P, BANK], F32, name="xw_bank%d" % c) for c in range(BANKS)]
-            for g in range(PASSES):
-                for c in range(BANKS):
-                    nc.tensor.matmul_mx(
-                        out=xw_banks[c][:],
-                        lhsT=x_codes[:, g, :].bitcast(FP8X4),
-                        lhsT_scale=x_scales[:, g, :],
-                        rhs=words[g][:, 2 * c * BANK : 2 * (c + 1) * BANK].bitcast(FP4X4),
-                        rhs_scale=planes[:, g, c * BANK : (c + 1) * BANK],
-                        start=(g == 0),
-                        stop=(g == PASSES - 1),
-                    )
+            for g, c in pass_order(r):
+                nc.tensor.matmul_mx(
+                    out=xw_banks[c][:],
+                    lhsT=x_codes[:, g, :].bitcast(FP8X4),
+                    lhsT_scale=x_scales[:, g, :],
+                    rhs=words[g, c].bitcast(FP4X4),
+                    rhs_scale=planes[:, g, c * BANK : (c + 1) * BANK],
+                    start=(g == 0),
+                    stop=(g == PASSES - 1),
+                )
 
             if r + EARLY < RANGES:
                 loaded.append(load_range(nc, keep, weight_words, weight_scales, r + EARLY, planes))
@@ -162,18 +173,25 @@ def tile_gcn_layer_w_e_kernel(tc, x, weight_words, weight_scales, out):
                 copy = nc.vector.tensor_copy if c % 2 == 0 else nc.scalar.copy
                 first = r * RANGE + c * BANK
                 xw = stage.tile([P, PER_PARTITION, P], F32, name="xw%d" % c)
-                copy(out=xw[:], in_=xw_banks[c][:].rearrange("p (m t) -> p t m", t=PER_PARTITION))
-                y_bank = psum.tile([P, PER_PARTITION, TOKENS], F32, name="y_bank%d" % c)
+                by_t = xw_banks[c][:].rearrange("p (m t) -> p t m", t=PER_PARTITION)
                 for t in range(PER_PARTITION):
-                    nc.tensor.matmul(out=y_bank[:, t, :], lhsT=xw[:, t, :], rhs=graph[:], start=True, stop=True)
-                y = keep.tile([P, BATCH, PER_PARTITION, CELLS], F32, name="y%d_%d" % (r, c))
-                copy(out=y[:], in_=y_bank[:].rearrange("m t (b s) -> m b t s", b=BATCH))
-                waiting.append((first, y))
+                    copy(out=xw[:, t, :], in_=by_t[:, t, :])
+                last = r == RANGES - 1 and c == BANKS - 1
+                share = PER_PARTITION // 2 if last else PER_PARTITION
+                to = out[:, first : first + BANK].rearrange("b (m t) i j -> m b t (i j)", t=PER_PARTITION)
+                for h, t0 in enumerate(range(0, PER_PARTITION, share)):
+                    y_bank = psum.tile([P, share, TOKENS], F32, name="y_bank%d" % ((c + h + 1) % 2 if last else c))
+                    for t in range(share):
+                        nc.tensor.matmul(
+                            out=y_bank[:, t, :], lhsT=xw[:, t0 + t, :], rhs=graph[:], start=True, stop=True
+                        )
+                    y = keep.tile([P, BATCH, share, CELLS], F32, name="y%d_%d_%d" % (r, c, h))
+                    leave = (nc.vector.tensor_copy, nc.scalar.copy)[h] if last else copy
+                    leave(out=y[:], in_=y_bank[:].rearrange("m t (b s) -> m b t s", b=BATCH))
+                    queue = nc.scalar if last and h == 1 else nc.sync
+                    waiting.append((queue, to[:, :, t0 : t0 + share, :].rearrange("m b t s -> m b (t s)"), y))
 
             if len(loaded) == RANGES:
-                for first, y in waiting:
-                    nc.sync.dma_start(
-                        out=out[:, first : first + BANK].rearrange("b (m t) i j -> m b (t i j)", t=PER_PARTITION),
-                        in_=y[:].rearrange("m b t s -> m b (t s)"),
-                    )
+                for queue, to, y in waiting:
+                    queue.dma_start(out=to, in_=y[:].rearrange("m b t s -> m b (t s)"))
                 waiting.clear()

@@ -55,12 +55,12 @@ def zero_planes(nc, keep, slot):
 def load_range(nc, keep, weight_words, weight_scales, r, planes):
     cols = slice(r * RANGE, (r + 1) * RANGE)
     rows = weight_scales.rearrange("g q n -> q g n")
-    for quadrant in range(2):
+    for half in range(2):
+        passes = slice(half * HALF, (half + 1) * HALF)
         for row in range(4):
-            q = 4 * quadrant + row
             nc.sync.dma_start(
-                out=planes[32 * quadrant + row : P : 64, :, :].bitcast(I32),
-                in_=rows[q : SCALE_ROWS : 8, :, cols].bitcast(I32),
+                out=planes[row : P : 32, passes, :].bitcast(I32),
+                in_=rows[row : SCALE_ROWS : 4, passes, cols].bitcast(I32),
             )
     words = {}
     for g, banks in load_order(r):

@@ -27,6 +27,7 @@ PER_PARTITION = BANK // P
 SCALE_ROWS = K_PASS // 32
 EARLY = 2
 SPLIT = 2
+SHORT = 2
 INNER = 3
 
 FLOPS = 2 * TOKENS * C_IN * C_OUT + 2 * TOKENS * TOKENS * C_OUT
@@ -55,8 +56,7 @@ def zero_planes(nc, keep, slot):
 def load_range(nc, keep, weight_words, weight_scales, r, planes):
     cols = slice(r * RANGE, (r + 1) * RANGE)
     rows = weight_scales.rearrange("g q n -> q g n")
-    for half in range(2):
-        passes = slice(half * HALF, (half + 1) * HALF)
+    for passes in (slice(0, SHORT), slice(SHORT, PASSES)):
         for row in range(4):
             nc.sync.dma_start(
                 out=planes[row : P : 32, passes, :].bitcast(I32),

@@ -20,15 +20,16 @@ TOKENS = BATCH * CELLS
 PASSES = C_IN // K_PASS
 HALF = PASSES // 2
 BANK = 512
-RANGE = 1024
-RANGES = C_OUT // RANGE
-BANKS = RANGE // BANK
+WIDE = 4
+NARROW = 2
 PER_PARTITION = BANK // P
 SCALE_ROWS = K_PASS // 32
-EARLY = 2
+QUADRANT_ROWS = 4
 SPLIT = 2
-SHORT = 2
 INNER = 3
+IMAGES = PER_PARTITION * BATCH
+PITCH = 16
+LEFT = 4
 
 FLOPS = 2 * TOKENS * C_IN * C_OUT + 2 * TOKENS * TOKENS * C_OUT
 
@@ -47,41 +48,25 @@ def box_sum(nc, pool, images, count):
     return box
 
 
-def zero_planes(nc, keep, slot):
-    planes = keep.tile([P, PASSES, RANGE], U8, name="planes%d" % slot, align_bytes=64)
-    nc.vector.memset(planes[:].bitcast(I32), 0)
-    return planes
-
-
-def load_range(nc, keep, weight_words, weight_scales, r, planes):
-    cols = slice(r * RANGE, (r + 1) * RANGE)
+def load_scales(nc, planes, weight_scales, first_pass, first, short):
+    count, width = planes.shape[1], planes.shape[2]
     rows = weight_scales.rearrange("g q n -> q g n")
-    for passes in (slice(0, SHORT), slice(SHORT, PASSES)):
-        for row in range(4):
+    for passes in (slice(0, short), slice(short, count)):
+        from_passes = slice(first_pass + passes.start, first_pass + passes.stop)
+        for row in range(QUADRANT_ROWS):
             nc.sync.dma_start(
                 out=planes[row : P : 32, passes, :].bitcast(I32),
-                in_=rows[row : SCALE_ROWS : 4, passes, cols].bitcast(I32),
+                in_=rows[row : SCALE_ROWS : QUADRANT_ROWS, from_passes, first : first + width].bitcast(I32),
             )
-    words = {}
-    for g, banks in load_order(r):
-        width = 2 * BANK * len(banks)
-        start = 2 * (r * RANGE + banks[0] * BANK)
-        piece = keep.tile([P, width], U8, name="words%d_%d_%d" % (r, g, banks[0]), align_bytes=64)
-        nc.sync.dma_start(out=piece[:].bitcast(I32), in_=weight_words[g, :, start : start + width].bitcast(I32))
-        for i, c in enumerate(banks):
-            words[g, c] = piece[:, 2 * i * BANK : 2 * (i + 1) * BANK]
-    return planes, words
 
 
-def load_order(r):
-    whole = PASSES - (SPLIT if r == RANGES - 1 else 0)
-    return [(g, list(range(BANKS))) for g in range(whole)] + [
-        (g, [c]) for c in range(BANKS) for g in range(whole, PASSES)
-    ]
-
-
-def pass_order(r):
-    return [(g, c) for g, banks in load_order(r) for c in banks]
+def load_words(nc, keep, weight_words, g, first, banks, words):
+    width = 2 * BANK * len(banks)
+    start = 2 * (first + banks[0] * BANK)
+    piece = keep.tile([P, width], U8, name="words%d_%d" % (g, start), align_bytes=64)
+    nc.sync.dma_start(out=piece[:].bitcast(I32), in_=weight_words[g, :, start : start + width].bitcast(I32))
+    for i, c in enumerate(banks):
+        words[g, c] = piece[:, 2 * i * BANK : 2 * (i + 1) * BANK]
 
 
 def tile_gcn_layer_w_e_kernel(tc, x, weight_words, weight_scales, out):
@@ -90,7 +75,7 @@ def tile_gcn_layer_w_e_kernel(tc, x, weight_words, weight_scales, out):
         ctx.enter_context(tc.manual_schedule())
         keep = ctx.enter_context(tc.tile_pool(name="keep", bufs=1))
         stage = ctx.enter_context(tc.tile_pool(name="stage", bufs=2))
-        psum = ctx.enter_context(tc.psum_pool(name="psum", bufs=2))
+        psum = ctx.enter_context(tc.psum_pool(name="psum", bufs=1))
 
         x_raw = keep.tile([P, BATCH, PASSES, PACK * CELLS], BF16, name="x_raw")
         for half in range(2):
@@ -100,11 +85,31 @@ def tile_gcn_layer_w_e_kernel(tc, x, weight_words, weight_scales, out):
                     out=x_raw[:, b, passes, :],
                     in_=x[b].rearrange("(g p t) i j -> p g (t i j)", g=PASSES, p=P, t=PACK)[:, passes, :],
                 )
-        zeroed = [zero_planes(nc, keep, slot) for slot in range(EARLY)]
-        loaded = [load_range(nc, keep, weight_words, weight_scales, r, zeroed[r]) for r in range(EARLY)]
+        slots = [keep.tile([P, HALF * WIDE * BANK], U8, name="slot%d" % i, align_bytes=64) for i in range(2)]
+        for slot in slots:
+            nc.vector.memset(slot[:].bitcast(I32), 0)
+        wide_planes = [slot[:].rearrange("p (g n) -> p g n", g=HALF) for slot in slots]
+        narrow_planes = [slot[:].rearrange("p (g n) -> p g n", g=PASSES) for slot in slots]
+        wide_words = {}
+        for half in range(2):
+            load_scales(nc, wide_planes[half], weight_scales, half * HALF, 0, 1)
+            for g in range(half * HALF, (half + 1) * HALF):
+                load_words(nc, keep, weight_words, g, 0, list(range(WIDE)), wide_words)
+
+        def load_narrow(r):
+            first = (WIDE + r * NARROW) * BANK
+            words = {}
+            load_scales(nc, narrow_planes[r], weight_scales, 0, first, 2)
+            whole = PASSES - (SPLIT if r == 1 else 0)
+            for g in range(whole):
+                load_words(nc, keep, weight_words, g, first, list(range(NARROW)), words)
+            for c in range(NARROW):
+                for g in range(whole, PASSES):
+                    load_words(nc, keep, weight_words, g, first, [c], words)
+            return words
 
         identity = keep.tile([P, TOKENS], F32, name="identity")
-        dinv = keep.tile([P, BATCH, GRID, GRID], F32, name="dinv")
+        dinv = keep.tile([P, IMAGES, GRID, GRID], F32, name="dinv")
         nc.gpsimd.memset(dinv[:], 1.0)
         make_identity(nc, identity[:])
         warm = keep.tile([P, 1], F32, name="warm")
@@ -144,54 +149,130 @@ def tile_gcn_layer_w_e_kernel(tc, x, weight_words, weight_scales, out):
         nc.vector.tensor_scalar_mul(
             out=dinv[:, :, :, 0 : GRID : GRID - 1], in0=dinv[:, :, :, 0 : GRID : GRID - 1], scalar1=border
         )
-        dinv_flat = dinv[:].rearrange("p b i j -> p (b i j)")
+        dinv_flat = dinv[:, :BATCH].rearrange("p b i j -> p (b i j)")
         own = keep.tile([P, TOKENS], F32, name="own")
         nc.vector.tensor_mul(out=own[:], in0=identity[:], in1=dinv_flat)
+        dinv_own = keep.tile([P, 1], F32, name="dinv_own")
+        nc.vector.reduce_sum(out=dinv_own[:], in_=own[:], axis=mybir.AxisListType.X)
         box = box_sum(nc, keep, own[:], BATCH)
         graph = keep.tile([P, TOKENS], F32, name="graph")
         nc.vector.tensor_mul(out=graph[:], in0=box[:].rearrange("p b s -> p (b s)"), in1=dinv_flat)
 
+        wide_images = [keep.tile([P, IMAGES * GRID, PITCH], F32, name="wide%d" % c) for c in range(WIDE)]
+        tall_images = [keep.tile([P, IMAGES, GRID + 2, GRID], F32, name="tall%d" % c) for c in range(WIDE)]
+        for c in range(WIDE):
+            nc.vector.memset(wide_images[c][:], 0.0)
+            nc.vector.memset(tall_images[c][:], 0.0)
+
         waiting = []
-        for r in range(RANGES):
-            planes, words = loaded[r]
-            xw_banks = [psum.tile([P, BANK], F32, name="xw_bank%d" % c) for c in range(BANKS)]
-            for g, c in pass_order(r):
-                nc.tensor.matmul_mx(
-                    out=xw_banks[c][:],
-                    lhsT=x_codes[:, g, :].bitcast(FP8X4),
-                    lhsT_scale=x_scales[:, g, :],
-                    rhs=words[g, c].bitcast(FP4X4),
-                    rhs_scale=planes[:, g, c * BANK : (c + 1) * BANK],
-                    start=(g == 0),
-                    stop=(g == PASSES - 1),
+
+        def mx_pass(bank, g, words, plane):
+            nc.tensor.matmul_mx(
+                out=bank[:],
+                lhsT=x_codes[:, g, :].bitcast(FP8X4),
+                lhsT_scale=x_scales[:, g, :],
+                rhs=words.bitcast(FP4X4),
+                rhs_scale=plane,
+                start=(g == 0),
+                stop=(g == PASSES - 1),
+            )
+
+        def by_piece(bank):
+            return bank[:].rearrange("p (m t) -> p t m", t=PER_PARTITION)
+
+        def place(first, t0, share):
+            to = out[:, first : first + BANK].rearrange("b (m t) i j -> m b t (i j)", t=PER_PARTITION)
+            return to[:, :, t0 : t0 + share, :].rearrange("m b t s -> m b (t s)")
+
+        def result(first, t0, share):
+            return keep.tile([P, BATCH, share, CELLS], F32, name="y%d_%d" % (first, t0))
+
+        banks = [psum.tile([P, BANK], F32, name="bank%d" % c) for c in range(WIDE)]
+        narrow_words = []
+        for half in range(2):
+            for g in range(half * HALF, (half + 1) * HALF):
+                for c in range(WIDE):
+                    mx_pass(
+                        banks[c], g, wide_words[g, c], wide_planes[half][:, g % HALF, c * BANK : (c + 1) * BANK]
+                    )
+            narrow_words.append(load_narrow(half))
+        turned = []
+        for c in range(WIDE):
+            xw = stage.tile([P, PER_PARTITION, P], F32, name="xw_wide%d" % (c % 2))
+            if c % 2 == 0:
+                nc.scalar.activation(
+                    out=xw[:], in_=by_piece(banks[c]), func=mybir.ActivationFunctionType.Copy, scale=dinv_own[:]
                 )
+            else:
+                nc.vector.tensor_scalar_mul(out=xw[:], in0=by_piece(banks[c]), scalar1=dinv_own[:])
+            turned.append(psum.tile([P, PER_PARTITION, TOKENS], F32, name="bank%d" % (WIDE + c)))
+            for t in range(PER_PARTITION):
+                nc.tensor.transpose(turned[c][:, t, :], xw[:, t, :], identity[:])
+        for c in range(WIDE):
+            nc.scalar.copy(
+                out=wide_images[c][:, :, LEFT : LEFT + GRID],
+                in_=turned[c][:].rearrange("m t (r j) -> m (t r) j", j=GRID),
+            )
 
-            if r + EARLY < RANGES:
-                loaded.append(load_range(nc, keep, weight_words, weight_scales, r + EARLY, planes))
+        def smooth_by_vector(pair):
+            pairs, boxes, ys = {}, {}, {}
+            for c in pair:
+                wide = wide_images[c]
+                pairs[c] = stage.tile([P, IMAGES * GRID, GRID], F32, name="pair%d" % (c % 2))
+                nc.vector.tensor_add(
+                    out=pairs[c][:], in0=wide[:, :, LEFT - 1 : LEFT - 1 + GRID], in1=wide[:, :, LEFT : LEFT + GRID]
+                )
+            for c in pair:
+                nc.vector.tensor_add(
+                    out=tall_images[c][:, :, 1 : 1 + GRID, :],
+                    in0=pairs[c][:].rearrange("p (n i) j -> p n i j", i=GRID),
+                    in1=wide_images[c][:, :, LEFT + 1 : LEFT + 1 + GRID].rearrange("p (n i) j -> p n i j", i=GRID),
+                )
+            for c in pair:
+                tall = tall_images[c]
+                boxes[c] = stage.tile([P, IMAGES, GRID, GRID], F32, name="box%d" % (c % 2))
+                nc.vector.tensor_add(out=boxes[c][:], in0=tall[:, :, 0:GRID, :], in1=tall[:, :, 1 : 1 + GRID, :])
+            for c in pair:
+                nc.vector.tensor_add(
+                    out=boxes[c][:], in0=boxes[c][:], in1=tall_images[c][:, :, 2 : 2 + GRID, :]
+                )
+            for c in pair:
+                first = c * BANK
+                ys[c] = result(first, 0, PER_PARTITION)
+                nc.vector.tensor_mul(
+                    out=ys[c][:].rearrange("p b t s -> p t b s"),
+                    in0=boxes[c][:].rearrange("p (t b) i j -> p t b (i j)", b=BATCH),
+                    in1=dinv[:].rearrange("p (t b) i j -> p t b (i j)", b=BATCH),
+                )
+                waiting.append((nc.sync, place(first, 0, PER_PARTITION), ys[c]))
 
-            for c in range(BANKS):
-                copy = nc.vector.tensor_copy if c % 2 == 0 else nc.scalar.copy
-                first = r * RANGE + c * BANK
+        for r in range(2):
+            smooth_by_vector((2 * r, 2 * r + 1))
+            base = (WIDE + r * NARROW) * BANK
+            banks = [psum.tile([P, BANK], F32, name="bank%d" % (NARROW * r + c)) for c in range(NARROW)]
+            whole = PASSES - (SPLIT if r == 1 else 0)
+            order = [(g, c) for g in range(whole) for c in range(NARROW)]
+            order += [(g, c) for c in range(NARROW) for g in range(whole, PASSES)]
+            for g, c in order:
+                mx_pass(banks[c], g, narrow_words[r][g, c], narrow_planes[r][:, g, c * BANK : (c + 1) * BANK])
+            copies = (nc.scalar.copy, nc.vector.tensor_copy)
+            for c in range(NARROW):
                 xw = stage.tile([P, PER_PARTITION, P], F32, name="xw%d" % c)
-                by_t = xw_banks[c][:].rearrange("p (m t) -> p t m", t=PER_PARTITION)
                 for t in range(PER_PARTITION):
-                    copy(out=xw[:, t, :], in_=by_t[:, t, :])
-                last = r == RANGES - 1 and c == BANKS - 1
+                    copies[c](out=xw[:, t, :], in_=by_piece(banks[c])[:, t, :])
+                last = r == 1 and c == NARROW - 1
                 share = PER_PARTITION // 2 if last else PER_PARTITION
-                to = out[:, first : first + BANK].rearrange("b (m t) i j -> m b t (i j)", t=PER_PARTITION)
                 for h, t0 in enumerate(range(0, PER_PARTITION, share)):
-                    y_bank = psum.tile([P, share, TOKENS], F32, name="y_bank%d" % ((c + h + 1) % 2 if last else c))
+                    y_bank = psum.tile([P, share, TOKENS], F32, name="bank%d" % (WIDE + (NARROW * r + c) * (1 - h)))
                     for t in range(share):
                         nc.tensor.matmul(
                             out=y_bank[:, t, :], lhsT=xw[:, t0 + t, :], rhs=graph[:], start=True, stop=True
                         )
-                    y = keep.tile([P, BATCH, share, CELLS], F32, name="y%d_%d_%d" % (r, c, h))
-                    leave = (nc.vector.tensor_copy, nc.scalar.copy)[h] if last else copy
+                    y = result(base + c * BANK, t0, share)
+                    leave = (nc.vector.tensor_copy, nc.scalar.copy)[h] if last else nc.scalar.copy
                     leave(out=y[:], in_=y_bank[:].rearrange("m t (b s) -> m b t s", b=BATCH))
                     queue = nc.scalar if last and h == 1 else nc.sync
-                    waiting.append((queue, to[:, :, t0 : t0 + share, :].rearrange("m b t s -> m b (t s)"), y))
+                    waiting.append((queue, place(base + c * BANK, t0, share), y))
 
-            if len(loaded) == RANGES:
-                for queue, to, y in waiting:
-                    queue.dma_start(out=to, in_=y[:].rearrange("m b t s -> m b (t s)"))
-                waiting.clear()
+        for queue, to, y in waiting:
+            queue.dma_start(out=to, in_=y[:].rearrange("m b t s -> m b (t s)"))

from contextlib import ExitStack

import concourse.mybir as mybir
from concourse.masks import make_identity

F32 = mybir.dt.float32
BF16 = mybir.dt.bfloat16
I32 = mybir.dt.int32
U32 = mybir.dt.uint32
U8 = mybir.dt.uint8
FP8X4 = mybir.dt.float8_e4m3fn_x4
FP4X4 = mybir.dt.float4_e2m1fn_x4

P = 128
PACK = 4
K_PASS = P * PACK
BATCH, C_IN, GRID, C_OUT = 2, 4096, 8, 4096
CELLS = GRID * GRID
TOKENS = BATCH * CELLS
PASSES = C_IN // K_PASS
HALF = PASSES // 2
BANK = 512
WIDE = 4
NARROW = 2
PER_PARTITION = BANK // P
SCALE_ROWS = K_PASS // 32
QUADRANT_ROWS = 4
SPLIT = 2
INNER = 3
IMAGES = PER_PARTITION * BATCH
PITCH = 16
LEFT = 4

FLOPS = 2 * TOKENS * C_IN * C_OUT + 2 * TOKENS * TOKENS * C_OUT


def box_sum(nc, pool, images, count):
    by_row = images.rearrange("p (r j) -> p r j", j=GRID)
    row_sum = pool.tile([P, count * GRID, GRID], F32, name="row_sum")
    nc.vector.tensor_copy(out=row_sum[:], in_=by_row)
    nc.vector.tensor_add(out=row_sum[:, :, 1:], in0=row_sum[:, :, 1:], in1=by_row[:, :, : GRID - 1])
    nc.vector.tensor_add(out=row_sum[:, :, : GRID - 1], in0=row_sum[:, :, : GRID - 1], in1=by_row[:, :, 1:])
    by_image = row_sum[:].rearrange("p (n i) j -> p n (i j)", i=GRID)
    box = pool.tile([P, count, CELLS], F32, name="box")
    nc.vector.tensor_copy(out=box[:], in_=by_image)
    nc.vector.tensor_add(out=box[:, :, GRID:], in0=box[:, :, GRID:], in1=by_image[:, :, : CELLS - GRID])
    nc.vector.tensor_add(out=box[:, :, : CELLS - GRID], in0=box[:, :, : CELLS - GRID], in1=by_image[:, :, GRID:])
    return box


def load_scales(nc, planes, weight_scales, first_pass, first, short):
    count, width = planes.shape[1], planes.shape[2]
    rows = weight_scales.rearrange("g q n -> q g n")
    for passes in (slice(0, short), slice(short, count)):
        from_passes = slice(first_pass + passes.start, first_pass + passes.stop)
        for row in range(QUADRANT_ROWS):
            nc.sync.dma_start(
                out=planes[row : P : 32, passes, :].bitcast(I32),
                in_=rows[row : SCALE_ROWS : QUADRANT_ROWS, from_passes, first : first + width].bitcast(I32),
            )


def load_words(nc, keep, weight_words, g, first, banks, words):
    width = 2 * BANK * len(banks)
    start = 2 * (first + banks[0] * BANK)
    piece = keep.tile([P, width], U8, name="words%d_%d" % (g, start), align_bytes=64)
    nc.sync.dma_start(out=piece[:].bitcast(I32), in_=weight_words[g, :, start : start + width].bitcast(I32))
    for i, c in enumerate(banks):
        words[g, c] = piece[:, 2 * i * BANK : 2 * (i + 1) * BANK]


def tile_gcn_layer_w_e_kernel(tc, x, weight_words, weight_scales, out):
    nc = tc.nc
    with ExitStack() as ctx:
        ctx.enter_context(tc.manual_schedule())
        keep = ctx.enter_context(tc.tile_pool(name="keep", bufs=1))
        stage = ctx.enter_context(tc.tile_pool(name="stage", bufs=2))
        psum = ctx.enter_context(tc.psum_pool(name="psum", bufs=1))

        x_raw = keep.tile([P, BATCH, PASSES, PACK * CELLS], BF16, name="x_raw")
        for half in range(2):
            passes = slice(half * HALF, (half + 1) * HALF)
            for b in range(BATCH):
                nc.sync.dma_start(
                    out=x_raw[:, b, passes, :],
                    in_=x[b].rearrange("(g p t) i j -> p g (t i j)", g=PASSES, p=P, t=PACK)[:, passes, :],
                )
        slots = [keep.tile([P, HALF * WIDE * BANK], U8, name="slot%d" % i, align_bytes=64) for i in range(2)]
        for slot in slots:
            nc.vector.memset(slot[:].bitcast(I32), 0)
        wide_planes = [slot[:].rearrange("p (g n) -> p g n", g=HALF) for slot in slots]
        narrow_planes = [slot[:].rearrange("p (g n) -> p g n", g=PASSES) for slot in slots]
        wide_words = {}
        for half in range(2):
            load_scales(nc, wide_planes[half], weight_scales, half * HALF, 0, 1)
            for g in range(half * HALF, (half + 1) * HALF):
                load_words(nc, keep, weight_words, g, 0, list(range(WIDE)), wide_words)

        def load_narrow(r):
            first = (WIDE + r * NARROW) * BANK
            words = {}
            load_scales(nc, narrow_planes[r], weight_scales, 0, first, 2)
            whole = PASSES - (SPLIT if r == 1 else 0)
            for g in range(whole):
                load_words(nc, keep, weight_words, g, first, list(range(NARROW)), words)
            for c in range(NARROW):
                for g in range(whole, PASSES):
                    load_words(nc, keep, weight_words, g, first, [c], words)
            return words

        identity = keep.tile([P, TOKENS], F32, name="identity")
        dinv = keep.tile([P, IMAGES, GRID, GRID], F32, name="dinv")
        nc.gpsimd.memset(dinv[:], 1.0)
        make_identity(nc, identity[:])
        warm = keep.tile([P, 1], F32, name="warm")
        nc.scalar.copy(out=warm[:], in_=dinv[:, 0, 0, :1])

        grouped = keep.tile([P, PASSES, TOKENS, PACK], BF16, name="grouped", align_bytes=64)
        x_codes = keep.tile([P, PASSES, TOKENS], U32, name="x_codes", align_bytes=64)
        x_scales = keep.tile([P, PASSES, TOKENS], U8, name="x_scales", align_bytes=64)

        def regroup(copy, half, b):
            passes = slice(half * HALF, (half + 1) * HALF)
            copy(
                out=grouped[:, passes, b * CELLS : (b + 1) * CELLS, :],
                in_=x_raw[:, b, passes, :].rearrange("p g (t s) -> p g s t", t=PACK),
            )

        def quantise(half):
            passes = slice(half * HALF, (half + 1) * HALF)
            nc.vector.quantize_mx(
                out=x_codes[:, passes, :].rearrange("p g s -> p (g s)").bitcast(FP8X4),
                scales=x_scales[:, passes, :].rearrange("p g s -> p (g s)"),
                in_=grouped[:, passes, :, :].rearrange("p g s t -> p (g s t)"),
            )

        regroup(nc.vector.tensor_copy, 0, 0)
        regroup(nc.vector.tensor_copy, 0, 1)
        regroup(nc.scalar.copy, 1, 0)
        quantise(0)
        regroup(nc.vector.tensor_copy, 1, 1)
        quantise(1)

        border = (INNER / (INNER - 1)) ** 0.5
        nc.vector.tensor_scalar_mul(out=dinv[:], in0=dinv[:], scalar1=1.0 / INNER)
        nc.vector.tensor_scalar_mul(
            out=dinv[:, :, 0 : GRID : GRID - 1, :], in0=dinv[:, :, 0 : GRID : GRID - 1, :], scalar1=border
        )
        nc.vector.tensor_scalar_mul(
            out=dinv[:, :, :, 0 : GRID : GRID - 1], in0=dinv[:, :, :, 0 : GRID : GRID - 1], scalar1=border
        )
        dinv_flat = dinv[:, :BATCH].rearrange("p b i j -> p (b i j)")
        own = keep.tile([P, TOKENS], F32, name="own")
        nc.vector.tensor_mul(out=own[:], in0=identity[:], in1=dinv_flat)
        dinv_own = keep.tile([P, 1], F32, name="dinv_own")
        nc.vector.reduce_sum(out=dinv_own[:], in_=own[:], axis=mybir.AxisListType.X)
        box = box_sum(nc, keep, own[:], BATCH)
        graph = keep.tile([P, TOKENS], F32, name="graph")
        nc.vector.tensor_mul(out=graph[:], in0=box[:].rearrange("p b s -> p (b s)"), in1=dinv_flat)

        wide_images = [keep.tile([P, IMAGES * GRID, PITCH], F32, name="wide%d" % c) for c in range(WIDE)]
        tall_images = [keep.tile([P, IMAGES, GRID + 2, GRID], F32, name="tall%d" % c) for c in range(WIDE)]
        for c in range(WIDE):
            nc.vector.memset(wide_images[c][:], 0.0)
            nc.vector.memset(tall_images[c][:], 0.0)

        waiting = []

        def mx_pass(bank, g, words, plane):
            nc.tensor.matmul_mx(
                out=bank[:],
                lhsT=x_codes[:, g, :].bitcast(FP8X4),
                lhsT_scale=x_scales[:, g, :],
                rhs=words.bitcast(FP4X4),
                rhs_scale=plane,
                start=(g == 0),
                stop=(g == PASSES - 1),
            )

        def by_piece(bank):
            return bank[:].rearrange("p (m t) -> p t m", t=PER_PARTITION)

        def place(first, t0, share):
            to = out[:, first : first + BANK].rearrange("b (m t) i j -> m b t (i j)", t=PER_PARTITION)
            return to[:, :, t0 : t0 + share, :].rearrange("m b t s -> m b (t s)")

        def result(first, t0, share):
            return keep.tile([P, BATCH, share, CELLS], F32, name="y%d_%d" % (first, t0))

        banks = [psum.tile([P, BANK], F32, name="bank%d" % c) for c in range(WIDE)]
        narrow_words = []
        for half in range(2):
            for g in range(half * HALF, (half + 1) * HALF):
                for c in range(WIDE):
                    mx_pass(
                        banks[c], g, wide_words[g, c], wide_planes[half][:, g % HALF, c * BANK : (c + 1) * BANK]
                    )
            narrow_words.append(load_narrow(half))
        turned = []
        for c in range(WIDE):
            xw = stage.tile([P, PER_PARTITION, P], F32, name="xw_wide%d" % (c % 2))
            if c % 2 == 0:
                nc.scalar.activation(
                    out=xw[:], in_=by_piece(banks[c]), func=mybir.ActivationFunctionType.Copy, scale=dinv_own[:]
                )
            else:
                nc.vector.tensor_scalar_mul(out=xw[:], in0=by_piece(banks[c]), scalar1=dinv_own[:])
            turned.append(psum.tile([P, PER_PARTITION, TOKENS], F32, name="bank%d" % (WIDE + c)))
            for t in range(PER_PARTITION):
                nc.tensor.transpose(turned[c][:, t, :], xw[:, t, :], identity[:])
        for c in range(WIDE):
            nc.scalar.copy(
                out=wide_images[c][:, :, LEFT : LEFT + GRID],
                in_=turned[c][:].rearrange("m t (r j) -> m (t r) j", j=GRID),
            )

        def smooth_by_vector(pair):
            pairs, boxes, ys = {}, {}, {}
            for c in pair:
                wide = wide_images[c]
                pairs[c] = stage.tile([P, IMAGES * GRID, GRID], F32, name="pair%d" % (c % 2))
                nc.vector.tensor_add(
                    out=pairs[c][:], in0=wide[:, :, LEFT - 1 : LEFT - 1 + GRID], in1=wide[:, :, LEFT : LEFT + GRID]
                )
            for c in pair:
                nc.vector.tensor_add(
                    out=tall_images[c][:, :, 1 : 1 + GRID, :],
                    in0=pairs[c][:].rearrange("p (n i) j -> p n i j", i=GRID),
                    in1=wide_images[c][:, :, LEFT + 1 : LEFT + 1 + GRID].rearrange("p (n i) j -> p n i j", i=GRID),
                )
            for c in pair:
                tall = tall_images[c]
                boxes[c] = stage.tile([P, IMAGES, GRID, GRID], F32, name="box%d" % (c % 2))
                nc.vector.tensor_add(out=boxes[c][:], in0=tall[:, :, 0:GRID, :], in1=tall[:, :, 1 : 1 + GRID, :])
            for c in pair:
                nc.vector.tensor_add(
                    out=boxes[c][:], in0=boxes[c][:], in1=tall_images[c][:, :, 2 : 2 + GRID, :]
                )
            for c in pair:
                first = c * BANK
                ys[c] = result(first, 0, PER_PARTITION)
                nc.vector.tensor_mul(
                    out=ys[c][:].rearrange("p b t s -> p t b s"),
                    in0=boxes[c][:].rearrange("p (t b) i j -> p t b (i j)", b=BATCH),
                    in1=dinv[:].rearrange("p (t b) i j -> p t b (i j)", b=BATCH),
                )
                waiting.append((nc.sync, place(first, 0, PER_PARTITION), ys[c]))

        for r in range(2):
            smooth_by_vector((2 * r, 2 * r + 1))
            base = (WIDE + r * NARROW) * BANK
            banks = [psum.tile([P, BANK], F32, name="bank%d" % (NARROW * r + c)) for c in range(NARROW)]
            whole = PASSES - (SPLIT if r == 1 else 0)
            order = [(g, c) for g in range(whole) for c in range(NARROW)]
            order += [(g, c) for c in range(NARROW) for g in range(whole, PASSES)]
            for g, c in order:
                mx_pass(banks[c], g, narrow_words[r][g, c], narrow_planes[r][:, g, c * BANK : (c + 1) * BANK])
            copies = (nc.scalar.copy, nc.vector.tensor_copy)
            for c in range(NARROW):
                xw = stage.tile([P, PER_PARTITION, P], F32, name="xw%d" % c)
                for t in range(PER_PARTITION):
                    copies[c](out=xw[:, t, :], in_=by_piece(banks[c])[:, t, :])
                last = r == 1 and c == NARROW - 1
                share = PER_PARTITION // 2 if last else PER_PARTITION
                for h, t0 in enumerate(range(0, PER_PARTITION, share)):
                    y_bank = psum.tile([P, share, TOKENS], F32, name="bank%d" % (WIDE + (NARROW * r + c) * (1 - h)))
                    for t in range(share):
                        nc.tensor.matmul(
                            out=y_bank[:, t, :], lhsT=xw[:, t0 + t, :], rhs=graph[:], start=True, stop=True
                        )
                    y = result(base + c * BANK, t0, share)
                    leave = (nc.vector.tensor_copy, nc.scalar.copy)[h] if last else nc.scalar.copy
                    leave(out=y[:], in_=y_bank[:].rearrange("m t (b s) -> m b t s", b=BATCH))
                    queue = nc.scalar if last and h == 1 else nc.sync
                    waiting.append((queue, place(base + c * BANK, t0, share), y))

        for queue, to, y in waiting:
            queue.dma_start(out=to, in_=y[:].rearrange("m b t s -> m b (t s)"))
